import numpy as np
import ml_dtypes


def mxq(x, axis, fmt="e4m3"):
    dtype, down = {"e4m3": (ml_dtypes.float8_e4m3fn, 7), "e5m2": (ml_dtypes.float8_e5m2, 14)}[fmt]
    v = np.moveaxis(np.asarray(x, np.float32).astype(ml_dtypes.bfloat16).astype(np.float64), axis, -1)
    blocks = v.reshape(v.shape[:-1] + (-1, 32))
    amax = np.abs(blocks).max(-1, keepdims=True)
    byte = np.maximum(np.where(amax > 0, np.frexp(amax)[1] - 1 + 127, 0) - down, 1)
    scale = np.exp2(byte - 127.0)
    codes = (blocks / scale).astype(np.float32).astype(dtype).astype(np.float64)
    return np.moveaxis((codes * scale).reshape(v.shape), -1, axis)


WIDE = False


def mx_kscale(k):
    if not WIDE:
        return np.ones(k)
    levels = np.array([10, -10, 5, -5, 0])
    if k % 512:
        return np.exp2(np.random.permutation(np.resize(levels, k // 32))).repeat(32)
    a = np.empty((k // 512, 16))
    for p in range(k // 512):
        a[p, :8] = np.random.permutation(np.resize(levels, 8))
        for g in range(8):
            far = levels[np.abs(levels - a[p, g]) >= 10]
            a[p, g + 8] = far[np.random.randint(len(far))]
    return np.exp2(a.ravel()).repeat(32)


BF16 = ml_dtypes.bfloat16


def bf(x):
    return np.asarray(x, np.float32).astype(BF16)


def f64(x):
    return np.asarray(x).astype(np.float64)


B, N_EP, S, D, IN_DIM, L, K = 6, 3, 512, 256, 255, 512, 10


def setup_inputs():
    s, t = mx_kscale(S), mx_kscale(L)
    r = np.random.standard_normal
    g = r((B, S, S)) * 1.56
    a = np.exp(g - g.max(-1, keepdims=True))
    a = a / a.sum(-1, keepdims=True)
    return {"attn1": bf(a * s), "v1": bf(r((B, S, L)) * 4.0 / s[:, None] * t),
            "Wq2": bf(r((L, L)) * 4.0 / np.sqrt(L) / t[:, None]), "bq2": bf(r(L) * 0.2),
            "Wk2": bf(r((L, L)) * 4.0 / np.sqrt(L) / t[:, None]), "bk2": bf(r(L) * 0.2),
            "Wv2": bf(r((L, L)) * 3.2 / np.sqrt(L) / t[:, None]), "bv2": bf(r(L) * 0.2)}


def reference(attn1, v1, Wq2, bq2, Wk2, bk2, Wv2, bv2):
    h = np.maximum(f64(bf(mxq(f64(attn1), 2, "e4m3") @ mxq(f64(v1), 1, "e4m3"))), 0.0)
    hq = mxq(h, 2, "e4m3")
    q2 = (hq @ mxq(f64(Wq2), 0, "e4m3")) + f64(bq2)
    k2 = (hq @ mxq(f64(Wk2), 0, "e4m3")) + f64(bk2)
    v2 = (hq @ mxq(f64(Wv2), 0, "e4m3")) + f64(bv2)
    return q2, k2, v2

@@ -1,0 +1,228 @@
+from contextlib import ExitStack
+
+import concourse.mybir as mybir
+from concourse.masks import make_identity
+
+B, S, L = 6, 512, 512
+FLOPS = B * 4 * 2 * S * S * L
+
+F32 = mybir.dt.float32
+BF16 = mybir.dt.bfloat16
+U32 = mybir.dt.uint32
+U8 = mybir.dt.uint8
+FP8X4 = mybir.dt.float8_e4m3fn_x4
+RELU = mybir.ActivationFunctionType.Relu
+ADD = mybir.AluOpType.add
+
+P = 128
+PACK = 4
+NT = 4
+H_BANK_DTYPE = BF16
+
+
+def tile_perspectronencodernetwork_pa_kernel(tc, attn1, v1, Wq2, bq2, Wk2, bk2, Wv2, bv2, out_0, out_1, out_2):
+    nc = tc.nc
+    weights = (Wq2, Wk2, Wv2)
+    biases = (bq2, bk2, bv2)
+    outs = (out_0, out_1, out_2)
+
+    with ExitStack() as ctx:
+        keep = ctx.enter_context(tc.tile_pool(name="keep", bufs=1))
+        work = ctx.enter_context(tc.tile_pool(name="work", bufs=2))
+        stage = ctx.enter_context(tc.tile_pool(name="stage", bufs=6))
+        psum_t = ctx.enter_context(tc.psum_pool(name="psum_t", bufs=2))
+        psum_h = ctx.enter_context(tc.psum_pool(name="psum_h", bufs=2))
+        psum_o = ctx.enter_context(tc.psum_pool(name="psum_o", bufs=4))
+        ctx.enter_context(tc.manual_schedule())
+
+        ones = keep.tile([P, P], BF16, name="ones")
+        nc.vector.memset(ones[:], 1.0)
+        bias_rows = keep.tile([P, 3, L], BF16, name="bias_rows")
+        nc.vector.memset(bias_rows[:], 0.0)
+        ident = keep.tile([P, P], F32, name="ident")
+        make_identity(nc, ident[:])
+        warm = keep.tile([P, 1], F32, name="warm")
+        nc.scalar.activation(out=warm[:], in_=ones[:, 0:1], func=RELU)
+        bias_all = keep.tile([P, 3, L], F32, name="bias_all")
+
+        a_raw = [keep.tile([P, PACK, S], BF16, name="a_raw%d" % b) for b in range(B)]
+        v_raw = [keep.tile([P, PACK, L], BF16, name="v_raw%d" % b) for b in range(B)]
+        w_raw = [keep.tile([P, PACK, L], BF16, name="w_raw%d" % o) for o in range(3)]
+
+        def load_set(b):
+            nc.sync.dma_start(out=a_raw[b][:], in_=attn1[b].rearrange("(p j) k -> p j k", j=PACK))
+            nc.sync.dma_start(out=v_raw[b][:], in_=v1[b].rearrange("(p j) f -> p j f", j=PACK))
+
+        load_set(0)
+        for o in range(3):
+            nc.sync.dma_start(out=bias_rows[0:1, o, :], in_=biases[o].rearrange("(x n) -> x n", x=1))
+        for o in range(3):
+            nc.sync.dma_start(out=w_raw[o][:], in_=weights[o].rearrange("(p j) n -> p j n", j=PACK))
+        for b in range(1, B):
+            load_set(b)
+
+        live = {}
+
+        def transpose_attn(b):
+            words = a_raw[b][:].bitcast(F32)
+            for half in range(2):
+                xt = psum_t.tile([P, 2, 2, P], F32, tag="xt", name="xt%d_%d" % (b, half))
+                live["xt", b, half] = xt
+                for jj in range(2):
+                    for u in range(2):
+                        nc.tensor.transpose(xt[:, jj, u, :], words[:, 2 * half + jj, u : S // 2 : 2], ident[:])
+
+        def copy_attn(b):
+            ag = work.tile([P, NT, P, PACK], BF16, tag="ag", name="ag%d" % b, align_bytes=64)
+            live["ag", b] = ag
+            ag_words = ag[:].bitcast(F32)
+            for half in range(2):
+                nc.scalar.copy(
+                    out=ag_words[:, 2 * half : 2 * half + 2, :, :],
+                    in_=live["xt", b, half][:].rearrange("p j u r -> p j r u"),
+                )
+
+        def interleave_v(b, engine_copy):
+            vg = work.tile([P, PACK, P, PACK], BF16, tag="vg", name="vg%d" % b, align_bytes=64, bufs=3)
+            live["vg", b] = vg
+            engine_copy(out=vg[:], in_=v_raw[b][:].rearrange("p j (m t) -> p t m j", t=PACK))
+
+        def interleave_w(o, engine_copy):
+            wg = work.tile([P, L, PACK], BF16, tag="wg", name="wg%d" % o, align_bytes=64)
+            live["wg", o] = wg
+            engine_copy(out=wg[:], in_=w_raw[o][:].rearrange("p j n -> p n j"))
+
+        def quantize(kind, idx, pool, flat_in):
+            slot = kind if kind != "w" else "w%d" % idx
+            codes = pool.tile([P, S], U32, tag=slot + "_codes", name="%s_codes%d" % (kind, idx), align_bytes=64)
+            scales = pool.tile([P, S], U8, tag=slot + "_scales", name="%s_scales%d" % (kind, idx), align_bytes=64)
+            live[kind, idx] = (codes, scales)
+            nc.vector.quantize_mx(out=codes[:].bitcast(FP8X4), scales=scales[:], in_=flat_in)
+
+        def quantize_attn(b):
+            quantize("a", b, work, live["ag", b][:].rearrange("p j r t -> p (j r t)"))
+
+        def quantize_v(b):
+            quantize("v", b, work, live["vg", b][:].rearrange("p t m j -> p (t m j)"))
+
+        def quantize_w(o):
+            quantize("w", o, keep, live["wg", o][:].rearrange("p n j -> p (n j)"))
+
+        def quantize_h(b):
+            quantize("h", b, work, live["hg", b][:].rearrange("p j r t -> p (j r t)"))
+
+        def cols(i):
+            return slice(i * P, (i + 1) * P)
+
+        def stage1(b, j):
+            a_codes, a_scales = live["a", b]
+            v_codes, v_scales = live["v", b]
+            hp = psum_h.tile([P, PACK, P], H_BANK_DTYPE, tag="hp", name="hp%d_%d" % (b, j))
+            for t in range(PACK):
+                nc.tensor.matmul_mx(
+                    out=hp[:, t, :],
+                    lhsT=v_codes[:, cols(t)].bitcast(FP8X4),
+                    lhsT_scale=v_scales[:, cols(t)],
+                    rhs=a_codes[:, cols(j)].bitcast(FP8X4),
+                    rhs_scale=a_scales[:, cols(j)],
+                    start=True,
+                    stop=True,
+                )
+            if j == 0:
+                live["hg", b] = work.tile([P, NT, P, PACK], BF16, tag="hg", name="hg%d" % b, align_bytes=64)
+            nc.scalar.activation(out=live["hg", b][:, j, :, :], in_=hp[:].rearrange("p t r -> p r t"), func=RELU)
+
+        def project(b, o, j):
+            h_codes, h_scales = live["h", b]
+            w_codes, w_scales = live["w", o]
+            acc = psum_o.tile([P, L], F32, tag="acc", name="acc%d_%d_%d" % (b, o, j))
+            live["acc", b, o, j] = acc
+            nc.tensor.matmul_mx(
+                out=acc[:],
+                lhsT=h_codes[:, cols(j)].bitcast(FP8X4),
+                lhsT_scale=h_scales[:, cols(j)],
+                rhs=w_codes[:].bitcast(FP8X4),
+                rhs_scale=w_scales[:],
+                start=True,
+                stop=True,
+            )
+
+        def add_bias_and_store(b, o, j):
+            if j == 0:
+                live["st", b, o] = stage.tile([P, NT, L], F32, tag="st", name="st%d_%d" % (b, o))
+            st = live["st", b, o]
+            nc.vector.tensor_tensor(out=st[:, j, :], in0=live["acc", b, o, j][:], in1=bias_all[:, o, :], op=ADD)
+            pieces = 1 if b < B - 1 else (2 if o < 2 else 4)
+            per = NT // pieces
+            if j % per == per - 1:
+                rows = slice(j + 1 - per, j + 1)
+                nc.sync.dma_start(out=outs[o][b].rearrange("(p j) n -> p j n", j=NT)[:, rows, :], in_=st[:, rows, :])
+
+        transpose_attn(0)
+        for o in range(3):
+            bias_bank = psum_o.tile([P, L], F32, tag="acc", name="bias_bank%d" % o)
+            live["bias_bank", o] = bias_bank
+            nc.tensor.matmul(out=bias_bank[:], lhsT=ones[:], rhs=bias_rows[:, o, :], start=True, stop=True)
+        copy_attn(0)
+        interleave_v(0, nc.vector.tensor_copy)
+        quantize_attn(0)
+        quantize_v(0)
+        interleave_w(0, nc.scalar.copy)
+        interleave_w(1, nc.vector.tensor_copy)
+        quantize_w(0)
+        interleave_w(2, nc.vector.tensor_copy)
+        quantize_w(1)
+        for j in range(NT):
+            stage1(0, j)
+        for o in range(3):
+            nc.scalar.copy(out=bias_all[:, o, :], in_=live["bias_bank", o][:])
+        transpose_attn(1)
+        copy_attn(1)
+        quantize_h(0)
+        for k in range(4):
+            project(0, k // NT, k % NT)
+        quantize_w(2)
+        transpose_attn(2)
+        interleave_v(2, nc.scalar.copy)
+        copy_attn(2)
+
+        per_set = 3 * NT
+        for b in range(B):
+            if 0 < b < B - 1:
+                stage1(b + 1, 0)
+                stage1(b + 1, 1)
+            last = b + 2 >= B
+            k2, k3 = (1, 2) if last else (6, 7)
+            for k in range(per_set):
+                add_bias_and_store(b, k // NT, k % NT)
+                if k + 4 < per_set:
+                    project(b, (k + 4) // NT, (k + 4) % NT)
+                if b == 0 and k == 1:
+                    interleave_v(1, nc.vector.tensor_copy)
+                    quantize_attn(1)
+                    quantize_v(1)
+                    stage1(1, 0)
+                    stage1(1, 1)
+                if b + 1 < B and k == k2:
+                    stage1(b + 1, 2)
+                if b + 1 < B and k == k3:
+                    stage1(b + 1, 3)
+                if b + 3 < B and k == k3:
+                    transpose_attn(b + 3)
+                    interleave_v(b + 3, nc.scalar.copy)
+                    copy_attn(b + 3)
+                if last and b + 1 < B:
+                    if k == 9:
+                        quantize_h(b + 1)
+                        project(b + 1, 0, 0)
+                        project(b + 1, 0, 1)
+                    if k == 10:
+                        project(b + 1, 0, 2)
+                    if k == 11:
+                        project(b + 1, 0, 3)
+            if not last:
+                quantize_h(b + 1)
+                for j in range(NT):
+                    project(b + 1, 0, j)
+                quantize_v(b + 2)
+                quantize_attn(b + 2)

@@ -13,6 +13,7 @@ U8 = mybir.dt.uint8
 FP8X4 = mybir.dt.float8_e4m3fn_x4
 RELU = mybir.ActivationFunctionType.Relu
 ADD = mybir.AluOpType.add
+MULT = mybir.AluOpType.mult
 
 P = 128
 PACK = 4
@@ -87,10 +88,16 @@ def tile_perspectronencodernetwork_pa_kernel(tc, attn1, v1, Wq2, bq2, Wk2, bk2, 
             live["vg", b] = vg
             engine_copy(out=vg[:], in_=v_raw[b][:].rearrange("p j (m t) -> p t m j", t=PACK))
 
+        def gpsimd_copy(out, in_):
+            nc.gpsimd.tensor_scalar(out=out, in0=in_, scalar1=1.0, scalar2=0.0, op0=MULT, op1=ADD)
+
         def interleave_w(o, engine_copy):
             wg = work.tile([P, L, PACK], BF16, tag="wg", name="wg%d" % o, align_bytes=64)
             live["wg", o] = wg
-            engine_copy(out=wg[:], in_=w_raw[o][:].rearrange("p j n -> p n j"))
+            engine_copy(
+                out=wg[:].rearrange("p (c i) j -> p c j i", i=PACK),
+                in_=w_raw[o][:].rearrange("p j (c i) -> p c j i", i=PACK),
+            )
 
         def quantize(kind, idx, pool, flat_in):
             slot = kind if kind != "w" else "w%d" % idx
@@ -158,6 +165,9 @@ def tile_perspectronencodernetwork_pa_kernel(tc, attn1, v1, Wq2, bq2, Wk2, bk2, 
                 rows = slice(j + 1 - per, j + 1)
                 nc.sync.dma_start(out=outs[o][b].rearrange("(p j) n -> p j n", j=NT)[:, rows, :], in_=st[:, rows, :])
 
+        def copy_bias(o):
+            nc.scalar.copy(out=bias_all[:, o, :], in_=live["bias_bank", o][:])
+
         transpose_attn(0)
         for o in range(3):
             bias_bank = psum_o.tile([P, L], F32, tag="acc", name="bias_bank%d" % o)
@@ -168,20 +178,24 @@ def tile_perspectronencodernetwork_pa_kernel(tc, attn1, v1, Wq2, bq2, Wk2, bk2, 
         quantize_attn(0)
         quantize_v(0)
         interleave_w(0, nc.scalar.copy)
+        copy_bias(0)
         interleave_w(1, nc.vector.tensor_copy)
         quantize_w(0)
         interleave_w(2, nc.vector.tensor_copy)
         quantize_w(1)
         for j in range(NT):
             stage1(0, j)
-        for o in range(3):
-            nc.scalar.copy(out=bias_all[:, o, :], in_=live["bias_bank", o][:])
+        copy_bias(1)
+        copy_bias(2)
         transpose_attn(1)
         copy_attn(1)
+        quantize_w(2)
         quantize_h(0)
         for k in range(4):
             project(0, k // NT, k % NT)
-        quantize_w(2)
+        fence = keep.tile([P, 1], U32, name="fence")
+        nc.gpsimd.tensor_copy(out=fence[:], in_=live["h", 0][0][:, 0:1])
+        interleave_v(1, gpsimd_copy)
         transpose_attn(2)
         interleave_v(2, nc.scalar.copy)
         copy_attn(2)
@@ -197,10 +211,9 @@ def tile_perspectronencodernetwork_pa_kernel(tc, attn1, v1, Wq2, bq2, Wk2, bk2, 
                 add_bias_and_store(b, k // NT, k % NT)
                 if k + 4 < per_set:
                     project(b, (k + 4) // NT, (k + 4) % NT)
-                if b == 0 and k == 1:
-                    interleave_v(1, nc.vector.tensor_copy)
-                    quantize_attn(1)
+                if b == 0 and k == 4:
                     quantize_v(1)
+                    quantize_attn(1)
                     stage1(1, 0)
                     stage1(1, 1)
                 if b + 1 < B and k == k2:

@@ -12,6 +12,7 @@ U32 = mybir.dt.uint32
 U8 = mybir.dt.uint8
 FP8X4 = mybir.dt.float8_e4m3fn_x4
 RELU = mybir.ActivationFunctionType.Relu
+IDENTITY = mybir.ActivationFunctionType.Identity
 ADD = mybir.AluOpType.add
 MULT = mybir.AluOpType.mult
 
@@ -19,6 +20,8 @@ P = 128
 PACK = 4
 NT = 4
 H_BANK_DTYPE = BF16
+PIECES = (2, 2, 2, 2, 2, 4)
+TURNED = (2, 2, 2, 2, 2, 2)
 
 
 def tile_perspectronencodernetwork_pa_kernel(tc, attn1, v1, Wq2, bq2, Wk2, bk2, Wv2, bv2, out_0, out_1, out_2):
@@ -31,8 +34,7 @@ def tile_perspectronencodernetwork_pa_kernel(tc, attn1, v1, Wq2, bq2, Wk2, bk2, 
         keep = ctx.enter_context(tc.tile_pool(name="keep", bufs=1))
         work = ctx.enter_context(tc.tile_pool(name="work", bufs=2))
         stage = ctx.enter_context(tc.tile_pool(name="stage", bufs=6))
-        psum_t = ctx.enter_context(tc.psum_pool(name="psum_t", bufs=2))
-        psum_h = ctx.enter_context(tc.psum_pool(name="psum_h", bufs=2))
+        ring = ctx.enter_context(tc.psum_pool(name="ring", bufs=4))
         psum_o = ctx.enter_context(tc.psum_pool(name="psum_o", bufs=4))
         ctx.enter_context(tc.manual_schedule())
 
@@ -67,7 +69,7 @@ def tile_perspectronencodernetwork_pa_kernel(tc, attn1, v1, Wq2, bq2, Wk2, bk2, 
         def transpose_attn(b):
             words = a_raw[b][:].bitcast(F32)
             for half in range(2):
-                xt = psum_t.tile([P, 2, 2, P], F32, tag="xt", name="xt%d_%d" % (b, half))
+                xt = ring.tile([P, 2, 2, P], F32, tag="ring", name="xt%d_%d" % (b, half))
                 live["xt", b, half] = xt
                 for jj in range(2):
                     for u in range(2):
@@ -124,7 +126,7 @@ def tile_perspectronencodernetwork_pa_kernel(tc, attn1, v1, Wq2, bq2, Wk2, bk2, 
         def stage1(b, j):
             a_codes, a_scales = live["a", b]
             v_codes, v_scales = live["v", b]
-            hp = psum_h.tile([P, PACK, P], H_BANK_DTYPE, tag="hp", name="hp%d_%d" % (b, j))
+            hp = ring.tile([P, PACK, P], H_BANK_DTYPE, tag="ring", name="hp%d_%d" % (b, j))
             for t in range(PACK):
                 nc.tensor.matmul_mx(
                     out=hp[:, t, :],
@@ -139,31 +141,70 @@ def tile_perspectronencodernetwork_pa_kernel(tc, attn1, v1, Wq2, bq2, Wk2, bk2, 
                 live["hg", b] = work.tile([P, NT, P, PACK], BF16, tag="hg", name="hg%d" % b, align_bytes=64)
             nc.scalar.activation(out=live["hg", b][:, j, :, :], in_=hp[:].rearrange("p t r -> p r t"), func=RELU)
 
+        def width(b, o):
+            return L - P * TURNED[b] if o == 2 else L
+
         def project(b, o, j):
             h_codes, h_scales = live["h", b]
             w_codes, w_scales = live["w", o]
+            n = width(b, o)
             acc = psum_o.tile([P, L], F32, tag="acc", name="acc%d_%d_%d" % (b, o, j))
             live["acc", b, o, j] = acc
             nc.tensor.matmul_mx(
-                out=acc[:],
+                out=acc[:, 0:n],
                 lhsT=h_codes[:, cols(j)].bitcast(FP8X4),
                 lhsT_scale=h_scales[:, cols(j)],
-                rhs=w_codes[:].bitcast(FP8X4),
-                rhs_scale=w_scales[:],
+                rhs=w_codes[:, 0:n].bitcast(FP8X4),
+                rhs_scale=w_scales[:, 0:n],
                 start=True,
                 stop=True,
             )
 
-        def add_bias_and_store(b, o, j):
-            if j == 0:
+        def staging(b, o):
+            if ("st", b, o) not in live:
                 live["st", b, o] = stage.tile([P, NT, L], F32, tag="st", name="st%d_%d" % (b, o))
-            st = live["st", b, o]
-            nc.vector.tensor_tensor(out=st[:, j, :], in0=live["acc", b, o, j][:], in1=bias_all[:, o, :], op=ADD)
-            pieces = 1 if b < B - 1 else (2 if o < 2 else 4)
+            return live["st", b, o]
+
+        def add_bias_and_store(b, o, j):
+            st = staging(b, o)
+            n = width(b, o)
+            nc.vector.tensor_tensor(out=st[:, j, 0:n], in0=live["acc", b, o, j][:, 0:n], in1=bias_all[:, o, 0:n], op=ADD)
+            pieces = PIECES[b]
             per = NT // pieces
             if j % per == per - 1:
                 rows = slice(j + 1 - per, j + 1)
                 nc.sync.dma_start(out=outs[o][b].rearrange("(p j) n -> p j n", j=NT)[:, rows, :], in_=st[:, rows, :])
+
+        def turned_tiles(b):
+            return range(NT - TURNED[b], NT)
+
+        def project_turned(b, c):
+            h_codes, h_scales = live["h", b]
+            w_codes, w_scales = live["w", 2]
+            bank = ring.tile([P, S], F32, tag="ring", name="tp%d_%d" % (b, c))
+            nc.tensor.matmul_mx(
+                out=bank[:],
+                lhsT=w_codes[:, cols(c)].bitcast(FP8X4),
+                lhsT_scale=w_scales[:, cols(c)],
+                rhs=h_codes[:].bitcast(FP8X4),
+                rhs_scale=h_scales[:],
+                start=True,
+                stop=True,
+            )
+            ot = work.tile([P, S], F32, tag="ot", name="ot%d_%d" % (b, c), bufs=4)
+            live["ot", b, c] = ot
+            nc.scalar.activation(out=ot[:], in_=bank[:], func=IDENTITY, bias=bias_col[:, c : c + 1])
+
+        def turn_back(b, c):
+            back = ring.tile([P, NT, P], F32, tag="ring", name="tb%d_%d" % (b, c))
+            for j in range(NT):
+                nc.tensor.transpose(back[:, j, :], live["ot", b, c][:, cols(j)], ident[:])
+            nc.scalar.copy(out=staging(b, 2)[:, :, cols(c)], in_=back[:])
+
+        fence = keep.tile([P, 1], U32, name="fence")
+
+        def gpsimd_waits_for(kind, idx):
+            nc.gpsimd.tensor_copy(out=fence[:], in_=live[kind, idx][0][:, 0:1])
 
         def copy_bias(o):
             nc.scalar.copy(out=bias_all[:, o, :], in_=live["bias_bank", o][:])
@@ -173,6 +214,10 @@ def tile_perspectronencodernetwork_pa_kernel(tc, attn1, v1, Wq2, bq2, Wk2, bk2, 
             bias_bank = psum_o.tile([P, L], F32, tag="acc", name="bias_bank%d" % o)
             live["bias_bank", o] = bias_bank
             nc.tensor.matmul(out=bias_bank[:], lhsT=ones[:], rhs=bias_rows[:, o, :], start=True, stop=True)
+        bias_col_bank = psum_o.tile([P, NT], F32, tag="acc", name="bias_col_bank")
+        for c in range(NT):
+            nc.tensor.matmul(out=bias_col_bank[:, c : c + 1], lhsT=bias_rows[:, 2, cols(c)], rhs=ones[:, 0:1], start=True, stop=True)
+        bias_col = keep.tile([P, NT], F32, name="bias_col")
         copy_attn(0)
         interleave_v(0, nc.vector.tensor_copy)
         quantize_attn(0)
@@ -187,17 +232,18 @@ def tile_perspectronencodernetwork_pa_kernel(tc, attn1, v1, Wq2, bq2, Wk2, bk2, 
             stage1(0, j)
         copy_bias(1)
         copy_bias(2)
+        nc.scalar.copy(out=bias_col[:], in_=bias_col_bank[:])
         transpose_attn(1)
         copy_attn(1)
         quantize_w(2)
         quantize_h(0)
         for k in range(4):
             project(0, k // NT, k % NT)
-        fence = keep.tile([P, 1], U32, name="fence")
-        nc.gpsimd.tensor_copy(out=fence[:], in_=live["h", 0][0][:, 0:1])
+        for c in turned_tiles(0):
+            project_turned(0, c)
+        gpsimd_waits_for("h", 0)
         interleave_v(1, gpsimd_copy)
         transpose_attn(2)
-        interleave_v(2, nc.scalar.copy)
         copy_attn(2)
 
         per_set = 3 * NT
@@ -206,23 +252,27 @@ def tile_perspectronencodernetwork_pa_kernel(tc, attn1, v1, Wq2, bq2, Wk2, bk2, 
                 stage1(b + 1, 0)
                 stage1(b + 1, 1)
             last = b + 2 >= B
-            k2, k3 = (1, 2) if last else (6, 7)
+            k2, k3 = (1, 2) if last else (4, 5)
             for k in range(per_set):
                 add_bias_and_store(b, k // NT, k % NT)
                 if k + 4 < per_set:
                     project(b, (k + 4) // NT, (k + 4) % NT)
+                if k == 1:
+                    for c in turned_tiles(b):
+                        turn_back(b, c)
                 if b == 0 and k == 4:
                     quantize_v(1)
                     quantize_attn(1)
+                    gpsimd_waits_for("a", 1)
+                    interleave_v(2, gpsimd_copy)
                     stage1(1, 0)
                     stage1(1, 1)
                 if b + 1 < B and k == k2:
                     stage1(b + 1, 2)
                 if b + 1 < B and k == k3:
                     stage1(b + 1, 3)
-                if b + 3 < B and k == k3:
+                if b + 3 < B and k == 7:
                     transpose_attn(b + 3)
-                    interleave_v(b + 3, nc.scalar.copy)
                     copy_attn(b + 3)
                 if last and b + 1 < B:
                     if k == 9:
@@ -233,9 +283,16 @@ def tile_perspectronencodernetwork_pa_kernel(tc, attn1, v1, Wq2, bq2, Wk2, bk2, 
                         project(b + 1, 0, 2)
                     if k == 11:
                         project(b + 1, 0, 3)
+                        for c in turned_tiles(b + 1):
+                            project_turned(b + 1, c)
             if not last:
                 quantize_h(b + 1)
                 for j in range(NT):
                     project(b + 1, 0, j)
+                for c in turned_tiles(b + 1):
+                    project_turned(b + 1, c)
                 quantize_v(b + 2)
                 quantize_attn(b + 2)
+                if b + 3 < B:
+                    gpsimd_waits_for("a", b + 2)
+                    interleave_v(b + 3, gpsimd_copy)

@@ -20,6 +20,7 @@ P = 128
 PACK = 4
 NT = 4
 H_BANK_DTYPE = BF16
+BACK_AT = 3
 PIECES = (2, 2, 2, 2, 2, 4)
 TURNED = (2, 2, 2, 2, 2, 2)
 
@@ -252,12 +253,12 @@ def tile_perspectronencodernetwork_pa_kernel(tc, attn1, v1, Wq2, bq2, Wk2, bk2, 
                 stage1(b + 1, 0)
                 stage1(b + 1, 1)
             last = b + 2 >= B
-            k2, k3 = (1, 2) if last else (4, 5)
+            k2, k3 = (5, 6) if b == 0 else (1, 2)
             for k in range(per_set):
                 add_bias_and_store(b, k // NT, k % NT)
                 if k + 4 < per_set:
                     project(b, (k + 4) // NT, (k + 4) % NT)
-                if k == 1:
+                if k == BACK_AT:
                     for c in turned_tiles(b):
                         turn_back(b, c)
                 if b == 0 and k == 4:

@@ -207,45 +207,38 @@ def tile_perspectronencodernetwork_pa_kernel(tc, attn1, v1, Wq2, bq2, Wk2, bk2, 
         def gpsimd_waits_for(kind, idx):
             nc.gpsimd.tensor_copy(out=fence[:], in_=live[kind, idx][0][:, 0:1])
 
-        def copy_bias(o):
-            nc.scalar.copy(out=bias_all[:, o, :], in_=live["bias_bank", o][:])
+        def spread_bias(o):
+            bias_bank = ring.tile([P, L], F32, tag="ring", name="bias_bank%d" % o)
+            nc.tensor.matmul(out=bias_bank[:], lhsT=ones[:], rhs=bias_rows[:, o, :], start=True, stop=True)
+            nc.scalar.copy(out=bias_all[:, o, :], in_=bias_bank[:])
 
         transpose_attn(0)
-        for o in range(3):
-            bias_bank = psum_o.tile([P, L], F32, tag="acc", name="bias_bank%d" % o)
-            live["bias_bank", o] = bias_bank
-            nc.tensor.matmul(out=bias_bank[:], lhsT=ones[:], rhs=bias_rows[:, o, :], start=True, stop=True)
-        bias_col_bank = psum_o.tile([P, NT], F32, tag="acc", name="bias_col_bank")
-        for c in range(NT):
-            nc.tensor.matmul(out=bias_col_bank[:, c : c + 1], lhsT=bias_rows[:, 2, cols(c)], rhs=ones[:, 0:1], start=True, stop=True)
-        bias_col = keep.tile([P, NT], F32, name="bias_col")
         copy_attn(0)
+        spread_bias(0)
+        spread_bias(1)
         interleave_v(0, nc.vector.tensor_copy)
-        quantize_attn(0)
         quantize_v(0)
-        interleave_w(0, nc.scalar.copy)
-        copy_bias(0)
-        interleave_w(1, nc.vector.tensor_copy)
-        quantize_w(0)
-        interleave_w(2, nc.vector.tensor_copy)
-        quantize_w(1)
+        quantize_attn(0)
+        interleave_w(0, nc.vector.tensor_copy)
         for j in range(NT):
             stage1(0, j)
-        copy_bias(1)
-        copy_bias(2)
-        nc.scalar.copy(out=bias_col[:], in_=bias_col_bank[:])
-        transpose_attn(1)
-        copy_attn(1)
-        quantize_w(2)
+        quantize_w(0)
+        interleave_w(1, nc.vector.tensor_copy)
         quantize_h(0)
         for k in range(4):
             project(0, k // NT, k % NT)
-        for c in turned_tiles(0):
-            project_turned(0, c)
-        gpsimd_waits_for("h", 0)
+        quantize_w(1)
+        gpsimd_waits_for("w", 1)
         interleave_v(1, gpsimd_copy)
-        transpose_attn(2)
-        copy_attn(2)
+        interleave_w(2, nc.scalar.copy)
+        transpose_attn(1)
+        copy_attn(1)
+        spread_bias(2)
+        bias_col_bank = ring.tile([P, NT], F32, tag="ring", name="bias_col_bank")
+        for c in range(NT):
+            nc.tensor.matmul(out=bias_col_bank[:, c : c + 1], lhsT=bias_rows[:, 2, cols(c)], rhs=ones[:, 0:1], start=True, stop=True)
+        bias_col = keep.tile([P, NT], F32, name="bias_col")
+        nc.scalar.copy(out=bias_col[:], in_=bias_col_bank[:])
 
         per_set = 3 * NT
         for b in range(B):
@@ -253,26 +246,32 @@ def tile_perspectronencodernetwork_pa_kernel(tc, attn1, v1, Wq2, bq2, Wk2, bk2, 
                 stage1(b + 1, 0)
                 stage1(b + 1, 1)
             last = b + 2 >= B
-            k2, k3 = (5, 6) if b == 0 else (1, 2)
+            k2, k3 = (4, 5) if b == 0 else (1, 2)
             for k in range(per_set):
                 add_bias_and_store(b, k // NT, k % NT)
                 if k + 4 < per_set:
                     project(b, (k + 4) // NT, (k + 4) % NT)
-                if k == BACK_AT:
+                if k == (BACK_AT if b > 0 else 7):
                     for c in turned_tiles(b):
                         turn_back(b, c)
-                if b == 0 and k == 4:
+                if b == 0 and k == 3:
+                    quantize_w(2)
                     quantize_v(1)
                     quantize_attn(1)
                     gpsimd_waits_for("a", 1)
                     interleave_v(2, gpsimd_copy)
+                    for c in turned_tiles(0):
+                        project_turned(0, c)
                     stage1(1, 0)
                     stage1(1, 1)
+                if b == 0 and k == 6:
+                    transpose_attn(2)
+                    copy_attn(2)
                 if b + 1 < B and k == k2:
                     stage1(b + 1, 2)
                 if b + 1 < B and k == k3:
                     stage1(b + 1, 3)
-                if b + 3 < B and k == 7:
+                if b + 3 < B and k == (7 if b > 0 else 9):
                     transpose_attn(b + 3)
                     copy_attn(b + 3)
                 if last and b + 1 < B:

@@ -21,6 +21,7 @@ PACK = 4
 NT = 4
 H_BANK_DTYPE = BF16
 BACK_AT = 3
+WARM = 6
 PIECES = (2, 2, 2, 2, 2, 4)
 TURNED = (2, 2, 2, 2, 2, 2)
 
@@ -41,6 +42,8 @@ def tile_perspectronencodernetwork_pa_kernel(tc, attn1, v1, Wq2, bq2, Wk2, bk2, 
 
         ones = keep.tile([P, P], BF16, name="ones")
         nc.vector.memset(ones[:], 1.0)
+        zeros = keep.tile([P, L], BF16, name="zeros")
+        nc.vector.memset(zeros[:], 0.0)
         bias_rows = keep.tile([P, 3, L], BF16, name="bias_rows")
         nc.vector.memset(bias_rows[:], 0.0)
         ident = keep.tile([P, P], F32, name="ident")
@@ -57,7 +60,10 @@ def tile_perspectronencodernetwork_pa_kernel(tc, attn1, v1, Wq2, bq2, Wk2, bk2, 
             nc.sync.dma_start(out=a_raw[b][:], in_=attn1[b].rearrange("(p j) k -> p j k", j=PACK))
             nc.sync.dma_start(out=v_raw[b][:], in_=v1[b].rearrange("(p j) f -> p j f", j=PACK))
 
-        load_set(0)
+        nc.sync.dma_start(out=v_raw[0][:], in_=v1[0].rearrange("(p j) f -> p j f", j=PACK))
+        for half in range(2):
+            rows = slice(2 * half, 2 * half + 2)
+            nc.sync.dma_start(out=a_raw[0][:, rows, :], in_=attn1[0].rearrange("(p j) k -> p j k", j=PACK)[:, rows, :])
         for o in range(3):
             nc.sync.dma_start(out=bias_rows[0:1, o, :], in_=biases[o].rearrange("(x n) -> x n", x=1))
         for o in range(3):
@@ -67,24 +73,23 @@ def tile_perspectronencodernetwork_pa_kernel(tc, attn1, v1, Wq2, bq2, Wk2, bk2, 
 
         live = {}
 
-        def transpose_attn(b):
+        def turn_attn(b, half):
             words = a_raw[b][:].bitcast(F32)
-            for half in range(2):
-                xt = ring.tile([P, 2, 2, P], F32, tag="ring", name="xt%d_%d" % (b, half))
-                live["xt", b, half] = xt
-                for jj in range(2):
-                    for u in range(2):
-                        nc.tensor.transpose(xt[:, jj, u, :], words[:, 2 * half + jj, u : S // 2 : 2], ident[:])
+            xt = ring.tile([P, 2, 2, P], F32, tag="ring", name="xt%d_%d" % (b, half))
+            for jj in range(2):
+                for u in range(2):
+                    nc.tensor.transpose(xt[:, jj, u, :], words[:, 2 * half + jj, u : S // 2 : 2], ident[:])
+            if half == 0:
+                live["ag", b] = work.tile([P, NT, P, PACK], BF16, tag="ag", name="ag%d" % b, align_bytes=64)
+            ag_words = live["ag", b][:].bitcast(F32)
+            nc.scalar.copy(out=ag_words[:, 2 * half : 2 * half + 2, :, :], in_=xt[:].rearrange("p j u r -> p j r u"))
+
+        def transpose_attn(b):
+            turn_attn(b, 0)
+            turn_attn(b, 1)
 
         def copy_attn(b):
-            ag = work.tile([P, NT, P, PACK], BF16, tag="ag", name="ag%d" % b, align_bytes=64)
-            live["ag", b] = ag
-            ag_words = ag[:].bitcast(F32)
-            for half in range(2):
-                nc.scalar.copy(
-                    out=ag_words[:, 2 * half : 2 * half + 2, :, :],
-                    in_=live["xt", b, half][:].rearrange("p j u r -> p j r u"),
-                )
+            return None
 
         def interleave_v(b, engine_copy):
             vg = work.tile([P, PACK, P, PACK], BF16, tag="vg", name="vg%d" % b, align_bytes=64, bufs=3)
@@ -102,15 +107,22 @@ def tile_perspectronencodernetwork_pa_kernel(tc, attn1, v1, Wq2, bq2, Wk2, bk2, 
                 in_=w_raw[o][:].rearrange("p j (c i) -> p c j i", i=PACK),
             )
 
-        def quantize(kind, idx, pool, flat_in):
+        def quantize(kind, idx, pool, flat_in, part=0, parts=1):
             slot = kind if kind != "w" else "w%d" % idx
-            codes = pool.tile([P, S], U32, tag=slot + "_codes", name="%s_codes%d" % (kind, idx), align_bytes=64)
-            scales = pool.tile([P, S], U8, tag=slot + "_scales", name="%s_scales%d" % (kind, idx), align_bytes=64)
-            live[kind, idx] = (codes, scales)
-            nc.vector.quantize_mx(out=codes[:].bitcast(FP8X4), scales=scales[:], in_=flat_in)
+            if (kind, idx) not in live:
+                codes = pool.tile([P, S], U32, tag=slot + "_codes", name="%s_codes%d" % (kind, idx), align_bytes=64)
+                scales = pool.tile([P, S], U8, tag=slot + "_scales", name="%s_scales%d" % (kind, idx), align_bytes=64)
+                live[kind, idx] = (codes, scales)
+            codes, scales = live[kind, idx]
+            w = S // parts
+            nc.vector.quantize_mx(
+                out=codes[:, part * w : (part + 1) * w].bitcast(FP8X4),
+                scales=scales[:, part * w : (part + 1) * w],
+                in_=flat_in[:, part * w * PACK : (part + 1) * w * PACK],
+            )
 
-        def quantize_attn(b):
-            quantize("a", b, work, live["ag", b][:].rearrange("p j r t -> p (j r t)"))
+        def quantize_attn(b, part=0, parts=1):
+            quantize("a", b, work, live["ag", b][:].rearrange("p j r t -> p (j r t)"), part, parts)
 
         def quantize_v(b):
             quantize("v", b, work, live["vg", b][:].rearrange("p t m j -> p (t m j)"))
@@ -212,16 +224,21 @@ def tile_perspectronencodernetwork_pa_kernel(tc, attn1, v1, Wq2, bq2, Wk2, bk2, 
             nc.tensor.matmul(out=bias_bank[:], lhsT=ones[:], rhs=bias_rows[:, o, :], start=True, stop=True)
             nc.scalar.copy(out=bias_all[:, o, :], in_=bias_bank[:])
 
-        transpose_attn(0)
-        copy_attn(0)
-        spread_bias(0)
-        spread_bias(1)
+        for i in range(WARM):
+            dummy = psum_o.tile([P, L], F32, tag="acc", name="dummy%d" % i)
+            nc.tensor.matmul(out=dummy[:], lhsT=ones[:], rhs=zeros[:], start=True, stop=True)
         interleave_v(0, nc.vector.tensor_copy)
         quantize_v(0)
-        quantize_attn(0)
+        turn_attn(0, 0)
+        turn_attn(0, 1)
+        quantize_attn(0, 0, 2)
+        stage1(0, 0)
+        stage1(0, 1)
+        quantize_attn(0, 1, 2)
         interleave_w(0, nc.vector.tensor_copy)
-        for j in range(NT):
-            stage1(0, j)
+        stage1(0, 2)
+        stage1(0, 3)
+        spread_bias(0)
         quantize_w(0)
         interleave_w(1, nc.vector.tensor_copy)
         quantize_h(0)
@@ -231,6 +248,7 @@ def tile_perspectronencodernetwork_pa_kernel(tc, attn1, v1, Wq2, bq2, Wk2, bk2, 
         gpsimd_waits_for("w", 1)
         interleave_v(1, gpsimd_copy)
         interleave_w(2, nc.scalar.copy)
+        spread_bias(1)
         transpose_attn(1)
         copy_attn(1)
         spread_bias(2)

@@ -224,9 +224,12 @@ def tile_perspectronencodernetwork_pa_kernel(tc, attn1, v1, Wq2, bq2, Wk2, bk2, 
             nc.tensor.matmul(out=bias_bank[:], lhsT=ones[:], rhs=bias_rows[:, o, :], start=True, stop=True)
             nc.scalar.copy(out=bias_all[:, o, :], in_=bias_bank[:])
 
-        for i in range(WARM):
-            dummy = psum_o.tile([P, L], F32, tag="acc", name="dummy%d" % i)
+        def keep_warm(name):
+            dummy = psum_o.tile([P, L], F32, tag="acc", name="dummy" + name)
             nc.tensor.matmul(out=dummy[:], lhsT=ones[:], rhs=zeros[:], start=True, stop=True)
+
+        for i in range(WARM):
+            keep_warm("%d" % i)
         interleave_v(0, nc.vector.tensor_copy)
         quantize_v(0)
         turn_attn(0, 0)
@@ -241,6 +244,8 @@ def tile_perspectronencodernetwork_pa_kernel(tc, attn1, v1, Wq2, bq2, Wk2, bk2, 
         spread_bias(0)
         quantize_w(0)
         interleave_w(1, nc.vector.tensor_copy)
+        for i in range(WARM):
+            keep_warm("h%d" % i)
         quantize_h(0)
         for k in range(4):
             project(0, k // NT, k % NT)
@@ -269,6 +274,8 @@ def tile_perspectronencodernetwork_pa_kernel(tc, attn1, v1, Wq2, bq2, Wk2, bk2, 
                 add_bias_and_store(b, k // NT, k % NT)
                 if k + 4 < per_set:
                     project(b, (k + 4) // NT, (k + 4) % NT)
+                elif 0 < b and not last:
+                    keep_warm("%d_%d" % (b, k))
                 if k == (BACK_AT if b > 0 else 7):
                     for c in turned_tiles(b):
                         turn_back(b, c)

@@ -91,10 +91,10 @@ def tile_perspectronencodernetwork_pa_kernel(tc, attn1, v1, Wq2, bq2, Wk2, bk2, 
         def copy_attn(b):
             return None
 
-        def interleave_v(b, engine_copy):
-            vg = work.tile([P, PACK, P, PACK], BF16, tag="vg", name="vg%d" % b, align_bytes=64, bufs=3)
-            live["vg", b] = vg
-            engine_copy(out=vg[:], in_=v_raw[b][:].rearrange("p j (m t) -> p t m j", t=PACK))
+        def interleave_v(b, engine_copy, t0=0, t1=PACK):
+            if ("vg", b) not in live:
+                live["vg", b] = work.tile([P, PACK, P, PACK], BF16, tag="vg", name="vg%d" % b, align_bytes=64, bufs=3)
+            engine_copy(out=live["vg", b][:, t0:t1], in_=v_raw[b][:].rearrange("p j (m t) -> p t m j", t=PACK)[:, t0:t1])
 
         def gpsimd_copy(out, in_):
             nc.gpsimd.tensor_scalar(out=out, in0=in_, scalar1=1.0, scalar2=0.0, op0=MULT, op1=ADD)
@@ -250,8 +250,9 @@ def tile_perspectronencodernetwork_pa_kernel(tc, attn1, v1, Wq2, bq2, Wk2, bk2, 
         for k in range(4):
             project(0, k // NT, k % NT)
         quantize_w(1)
+        interleave_v(1, nc.vector.tensor_copy, 0, 2)
         gpsimd_waits_for("w", 1)
-        interleave_v(1, gpsimd_copy)
+        interleave_v(1, gpsimd_copy, 2, 4)
         interleave_w(2, nc.scalar.copy)
         spread_bias(1)
         transpose_attn(1)
@@ -283,8 +284,9 @@ def tile_perspectronencodernetwork_pa_kernel(tc, attn1, v1, Wq2, bq2, Wk2, bk2, 
                     quantize_w(2)
                     quantize_v(1)
                     quantize_attn(1)
+                    interleave_v(2, nc.scalar.copy, 0, 1)
                     gpsimd_waits_for("a", 1)
-                    interleave_v(2, gpsimd_copy)
+                    interleave_v(2, gpsimd_copy, 1, 4)
                     for c in turned_tiles(0):
                         project_turned(0, c)
                     stage1(1, 0)

@@ -22,7 +22,9 @@ NT = 4
 H_BANK_DTYPE = BF16
 BACK_AT = 3
 WARM = 6
-PIECES = (2, 2, 2, 2, 2, 4)
+V0_SPLIT = 80
+HALVES = (2, 2)
+STORES = ((HALVES,) * 3,) * 5 + ((HALVES, HALVES, (2, 1, 1)),)
 TURNED = (2, 2, 2, 2, 2, 2)
 
 
@@ -64,10 +66,11 @@ def tile_perspectronencodernetwork_pa_kernel(tc, attn1, v1, Wq2, bq2, Wk2, bk2, 
         for half in range(2):
             rows = slice(2 * half, 2 * half + 2)
             nc.sync.dma_start(out=a_raw[0][:, rows, :], in_=attn1[0].rearrange("(p j) k -> p j k", j=PACK)[:, rows, :])
+        for o in range(2):
+            nc.sync.dma_start(out=w_raw[o][:], in_=weights[o].rearrange("(p j) n -> p j n", j=PACK))
         for o in range(3):
             nc.sync.dma_start(out=bias_rows[0:1, o, :], in_=biases[o].rearrange("(x n) -> x n", x=1))
-        for o in range(3):
-            nc.sync.dma_start(out=w_raw[o][:], in_=weights[o].rearrange("(p j) n -> p j n", j=PACK))
+        nc.sync.dma_start(out=w_raw[2][:], in_=weights[2].rearrange("(p j) n -> p j n", j=PACK))
         for b in range(1, B):
             load_set(b)
 
@@ -95,6 +98,11 @@ def tile_perspectronencodernetwork_pa_kernel(tc, attn1, v1, Wq2, bq2, Wk2, bk2, 
             if ("vg", b) not in live:
                 live["vg", b] = work.tile([P, PACK, P, PACK], BF16, tag="vg", name="vg%d" % b, align_bytes=64, bufs=3)
             engine_copy(out=live["vg", b][:, t0:t1], in_=v_raw[b][:].rearrange("p j (m t) -> p t m j", t=PACK)[:, t0:t1])
+
+        def interleave_v_columns(b, engine_copy, m0, m1):
+            if ("vg", b) not in live:
+                live["vg", b] = work.tile([P, PACK, P, PACK], BF16, tag="vg", name="vg%d" % b, align_bytes=64, bufs=3)
+            engine_copy(out=live["vg", b][:, :, m0:m1, :], in_=v_raw[b][:].rearrange("p j (m t) -> p t m j", t=PACK)[:, :, m0:m1, :])
 
         def gpsimd_copy(out, in_):
             nc.gpsimd.tensor_scalar(out=out, in0=in_, scalar1=1.0, scalar2=0.0, op0=MULT, op1=ADD)
@@ -181,11 +189,14 @@ def tile_perspectronencodernetwork_pa_kernel(tc, attn1, v1, Wq2, bq2, Wk2, bk2, 
         def add_bias_and_store(b, o, j):
             st = staging(b, o)
             n = width(b, o)
+            rows = None
             nc.vector.tensor_tensor(out=st[:, j, 0:n], in0=live["acc", b, o, j][:, 0:n], in1=bias_all[:, o, 0:n], op=ADD)
-            pieces = PIECES[b]
-            per = NT // pieces
-            if j % per == per - 1:
-                rows = slice(j + 1 - per, j + 1)
+            first = 0
+            for count in STORES[b][o]:
+                if first + count == j + 1:
+                    rows = slice(first, j + 1)
+                first += count
+            if rows is not None:
                 nc.sync.dma_start(out=outs[o][b].rearrange("(p j) n -> p j n", j=NT)[:, rows, :], in_=st[:, rows, :])
 
         def turned_tiles(b):
@@ -230,7 +241,8 @@ def tile_perspectronencodernetwork_pa_kernel(tc, attn1, v1, Wq2, bq2, Wk2, bk2, 
 
         for i in range(WARM):
             keep_warm("%d" % i)
-        interleave_v(0, nc.vector.tensor_copy)
+        interleave_v_columns(0, nc.vector.tensor_copy, 0, V0_SPLIT)
+        interleave_v_columns(0, nc.scalar.copy, V0_SPLIT, P)
         quantize_v(0)
         turn_attn(0, 0)
         turn_attn(0, 1)
@@ -242,16 +254,16 @@ def tile_perspectronencodernetwork_pa_kernel(tc, attn1, v1, Wq2, bq2, Wk2, bk2, 
         stage1(0, 2)
         stage1(0, 3)
         spread_bias(0)
-        quantize_w(0)
         interleave_w(1, nc.vector.tensor_copy)
+        quantize_w(0)
         for i in range(WARM):
             keep_warm("h%d" % i)
+        quantize_w(1)
         quantize_h(0)
         for k in range(4):
             project(0, k // NT, k % NT)
-        quantize_w(1)
         interleave_v(1, nc.vector.tensor_copy, 0, 2)
-        gpsimd_waits_for("w", 1)
+        gpsimd_waits_for("h", 0)
         interleave_v(1, gpsimd_copy, 2, 4)
         interleave_w(2, nc.scalar.copy)
         spread_bias(1)

@@ -52,7 +52,7 @@ def tile_perspectronencodernetwork_pa_kernel(tc, attn1, v1, Wq2, bq2, Wk2, bk2, 
         make_identity(nc, ident[:])
         warm = keep.tile([P, 1], F32, name="warm")
         nc.scalar.activation(out=warm[:], in_=ones[:, 0:1], func=RELU)
-        bias_all = keep.tile([P, 3, L], F32, name="bias_all")
+        bias_all = keep.tile([P, 3, L], BF16, name="bias_all")
 
         a_raw = [keep.tile([P, PACK, S], BF16, name="a_raw%d" % b) for b in range(B)]
         v_raw = [keep.tile([P, PACK, L], BF16, name="v_raw%d" % b) for b in range(B)]
@@ -230,10 +230,14 @@ def tile_perspectronencodernetwork_pa_kernel(tc, attn1, v1, Wq2, bq2, Wk2, bk2, 
         def gpsimd_waits_for(kind, idx):
             nc.gpsimd.tensor_copy(out=fence[:], in_=live[kind, idx][0][:, 0:1])
 
-        def spread_bias(o):
-            bias_bank = ring.tile([P, L], F32, tag="ring", name="bias_bank%d" % o)
-            nc.tensor.matmul(out=bias_bank[:], lhsT=ones[:], rhs=bias_rows[:, o, :], start=True, stop=True)
-            nc.scalar.copy(out=bias_all[:, o, :], in_=bias_bank[:])
+        def spread_bias(first, count):
+            bias_bank = ring.tile([P, count, L], BF16, tag="ring", name="bias_bank%d" % first)
+            for i in range(count):
+                nc.tensor.matmul(out=bias_bank[:, i, :], lhsT=ones[:], rhs=bias_rows[:, first + i, :], start=True, stop=True)
+            nc.scalar.copy(
+                out=bias_all[:, first : first + count, :].rearrange("p o n -> p (o n)").bitcast(F32),
+                in_=bias_bank[:].rearrange("p o n -> p (o n)").bitcast(F32),
+            )
 
         def keep_warm(name):
             dummy = psum_o.tile([P, L], F32, tag="acc", name="dummy" + name)
@@ -253,7 +257,7 @@ def tile_perspectronencodernetwork_pa_kernel(tc, attn1, v1, Wq2, bq2, Wk2, bk2, 
         interleave_w(0, nc.vector.tensor_copy)
         stage1(0, 2)
         stage1(0, 3)
-        spread_bias(0)
+        spread_bias(0, 2)
         interleave_w(1, nc.vector.tensor_copy)
         quantize_w(0)
         for i in range(WARM):
@@ -266,10 +270,9 @@ def tile_perspectronencodernetwork_pa_kernel(tc, attn1, v1, Wq2, bq2, Wk2, bk2, 
         gpsimd_waits_for("h", 0)
         interleave_v(1, gpsimd_copy, 2, 4)
         interleave_w(2, nc.scalar.copy)
-        spread_bias(1)
         transpose_attn(1)
         copy_attn(1)
-        spread_bias(2)
+        spread_bias(2, 1)
         bias_col_bank = ring.tile([P, NT], F32, tag="ring", name="bias_col_bank")
         for c in range(NT):
             nc.tensor.matmul(out=bias_col_bank[:, c : c + 1], lhsT=bias_rows[:, 2, cols(c)], rhs=ones[:, 0:1], start=True, stop=True)

@@ -22,6 +22,7 @@ NT = 4
 H_BANK_DTYPE = BF16
 BACK_AT = 3
 WARM = 6
+LATE = (1, 2, 3)
 V0_SPLIT = 80
 HALVES = (2, 2)
 STORES = ((HALVES,) * 3,) * 5 + ((HALVES, HALVES, (2, 1, 1)),)
@@ -290,9 +291,9 @@ def tile_perspectronencodernetwork_pa_kernel(tc, attn1, v1, Wq2, bq2, Wk2, bk2, 
                 add_bias_and_store(b, k // NT, k % NT)
                 if k + 4 < per_set:
                     project(b, (k + 4) // NT, (k + 4) % NT)
-                elif 0 < b and not last:
+                elif 0 < b and not last and b not in LATE:
                     keep_warm("%d_%d" % (b, k))
-                if k == (BACK_AT if b > 0 else 7):
+                if k == (BACK_AT if b > 0 and b not in LATE else 7):
                     for c in turned_tiles(b):
                         turn_back(b, c)
                 if b == 0 and k == 3:
@@ -313,6 +314,9 @@ def tile_perspectronencodernetwork_pa_kernel(tc, attn1, v1, Wq2, bq2, Wk2, bk2, 
                     stage1(b + 1, 2)
                 if b + 1 < B and k == k3:
                     stage1(b + 1, 3)
+                    if b in LATE:
+                        for c in turned_tiles(b):
+                            project_turned(b, c)
                 if b + 3 < B and k == (7 if b > 0 else 9):
                     transpose_attn(b + 3)
                     copy_attn(b + 3)
@@ -331,8 +335,9 @@ def tile_perspectronencodernetwork_pa_kernel(tc, attn1, v1, Wq2, bq2, Wk2, bk2, 
                 quantize_h(b + 1)
                 for j in range(NT):
                     project(b + 1, 0, j)
-                for c in turned_tiles(b + 1):
-                    project_turned(b + 1, c)
+                if b + 1 not in LATE:
+                    for c in turned_tiles(b + 1):
+                        project_turned(b + 1, c)
                 quantize_v(b + 2)
                 quantize_attn(b + 2)
                 if b + 3 < B:

from contextlib import ExitStack

import concourse.mybir as mybir
from concourse.masks import make_identity

B, S, L = 6, 512, 512
FLOPS = B * 4 * 2 * S * S * L

F32 = mybir.dt.float32
BF16 = mybir.dt.bfloat16
U32 = mybir.dt.uint32
U8 = mybir.dt.uint8
FP8X4 = mybir.dt.float8_e4m3fn_x4
RELU = mybir.ActivationFunctionType.Relu
IDENTITY = mybir.ActivationFunctionType.Identity
ADD = mybir.AluOpType.add
MULT = mybir.AluOpType.mult

P = 128
PACK = 4
NT = 4
H_BANK_DTYPE = BF16
BACK_AT = 3
WARM = 6
LATE = (1, 2, 3)
V0_SPLIT = 80
HALVES = (2, 2)
STORES = ((HALVES,) * 3,) * 5 + ((HALVES, HALVES, (2, 1, 1)),)
TURNED = (2, 2, 2, 2, 2, 2)


def tile_perspectronencodernetwork_pa_kernel(tc, attn1, v1, Wq2, bq2, Wk2, bk2, Wv2, bv2, out_0, out_1, out_2):
    nc = tc.nc
    weights = (Wq2, Wk2, Wv2)
    biases = (bq2, bk2, bv2)
    outs = (out_0, out_1, out_2)

    with ExitStack() as ctx:
        keep = ctx.enter_context(tc.tile_pool(name="keep", bufs=1))
        work = ctx.enter_context(tc.tile_pool(name="work", bufs=2))
        stage = ctx.enter_context(tc.tile_pool(name="stage", bufs=6))
        ring = ctx.enter_context(tc.psum_pool(name="ring", bufs=4))
        psum_o = ctx.enter_context(tc.psum_pool(name="psum_o", bufs=4))
        ctx.enter_context(tc.manual_schedule())

        ones = keep.tile([P, P], BF16, name="ones")
        nc.vector.memset(ones[:], 1.0)
        zeros = keep.tile([P, L], BF16, name="zeros")
        nc.vector.memset(zeros[:], 0.0)
        bias_rows = keep.tile([P, 3, L], BF16, name="bias_rows")
        nc.vector.memset(bias_rows[:], 0.0)
        ident = keep.tile([P, P], F32, name="ident")
        make_identity(nc, ident[:])
        warm = keep.tile([P, 1], F32, name="warm")
        nc.scalar.activation(out=warm[:], in_=ones[:, 0:1], func=RELU)
        bias_all = keep.tile([P, 3, L], BF16, name="bias_all")

        a_raw = [keep.tile([P, PACK, S], BF16, name="a_raw%d" % b) for b in range(B)]
        v_raw = [keep.tile([P, PACK, L], BF16, name="v_raw%d" % b) for b in range(B)]
        w_raw = [keep.tile([P, PACK, L], BF16, name="w_raw%d" % o) for o in range(3)]

        def load_set(b):
            nc.sync.dma_start(out=a_raw[b][:], in_=attn1[b].rearrange("(p j) k -> p j k", j=PACK))
            nc.sync.dma_start(out=v_raw[b][:], in_=v1[b].rearrange("(p j) f -> p j f", j=PACK))

        nc.sync.dma_start(out=v_raw[0][:], in_=v1[0].rearrange("(p j) f -> p j f", j=PACK))
        for half in range(2):
            rows = slice(2 * half, 2 * half + 2)
            nc.sync.dma_start(out=a_raw[0][:, rows, :], in_=attn1[0].rearrange("(p j) k -> p j k", j=PACK)[:, rows, :])
        for o in range(2):
            nc.sync.dma_start(out=w_raw[o][:], in_=weights[o].rearrange("(p j) n -> p j n", j=PACK))
        for o in range(3):
            nc.sync.dma_start(out=bias_rows[0:1, o, :], in_=biases[o].rearrange("(x n) -> x n", x=1))
        nc.sync.dma_start(out=w_raw[2][:], in_=weights[2].rearrange("(p j) n -> p j n", j=PACK))
        for b in range(1, B):
            load_set(b)

        live = {}

        def turn_attn(b, half):
            words = a_raw[b][:].bitcast(F32)
            xt = ring.tile([P, 2, 2, P], F32, tag="ring", name="xt%d_%d" % (b, half))
            for jj in range(2):
                for u in range(2):
                    nc.tensor.transpose(xt[:, jj, u, :], words[:, 2 * half + jj, u : S // 2 : 2], ident[:])
            if half == 0:
                live["ag", b] = work.tile([P, NT, P, PACK], BF16, tag="ag", name="ag%d" % b, align_bytes=64)
            ag_words = live["ag", b][:].bitcast(F32)
            nc.scalar.copy(out=ag_words[:, 2 * half : 2 * half + 2, :, :], in_=xt[:].rearrange("p j u r -> p j r u"))

        def transpose_attn(b):
            turn_attn(b, 0)
            turn_attn(b, 1)

        def copy_attn(b):
            return None

        def interleave_v(b, engine_copy, t0=0, t1=PACK):
            if ("vg", b) not in live:
                live["vg", b] = work.tile([P, PACK, P, PACK], BF16, tag="vg", name="vg%d" % b, align_bytes=64, bufs=3)
            engine_copy(out=live["vg", b][:, t0:t1], in_=v_raw[b][:].rearrange("p j (m t) -> p t m j", t=PACK)[:, t0:t1])

        def interleave_v_columns(b, engine_copy, m0, m1):
            if ("vg", b) not in live:
                live["vg", b] = work.tile([P, PACK, P, PACK], BF16, tag="vg", name="vg%d" % b, align_bytes=64, bufs=3)
            engine_copy(out=live["vg", b][:, :, m0:m1, :], in_=v_raw[b][:].rearrange("p j (m t) -> p t m j", t=PACK)[:, :, m0:m1, :])

        def gpsimd_copy(out, in_):
            nc.gpsimd.tensor_scalar(out=out, in0=in_, scalar1=1.0, scalar2=0.0, op0=MULT, op1=ADD)

        def interleave_w(o, engine_copy):
            wg = work.tile([P, L, PACK], BF16, tag="wg", name="wg%d" % o, align_bytes=64)
            live["wg", o] = wg
            engine_copy(
                out=wg[:].rearrange("p (c i) j -> p c j i", i=PACK),
                in_=w_raw[o][:].rearrange("p j (c i) -> p c j i", i=PACK),
            )

        def quantize(kind, idx, pool, flat_in, part=0, parts=1):
            slot = kind if kind != "w" else "w%d" % idx
            if (kind, idx) not in live:
                codes = pool.tile([P, S], U32, tag=slot + "_codes", name="%s_codes%d" % (kind, idx), align_bytes=64)
                scales = pool.tile([P, S], U8, tag=slot + "_scales", name="%s_scales%d" % (kind, idx), align_bytes=64)
                live[kind, idx] = (codes, scales)
            codes, scales = live[kind, idx]
            w = S // parts
            nc.vector.quantize_mx(
                out=codes[:, part * w : (part + 1) * w].bitcast(FP8X4),
                scales=scales[:, part * w : (part + 1) * w],
                in_=flat_in[:, part * w * PACK : (part + 1) * w * PACK],
            )

        def quantize_attn(b, part=0, parts=1):
            quantize("a", b, work, live["ag", b][:].rearrange("p j r t -> p (j r t)"), part, parts)

        def quantize_v(b):
            quantize("v", b, work, live["vg", b][:].rearrange("p t m j -> p (t m j)"))

        def quantize_w(o):
            quantize("w", o, keep, live["wg", o][:].rearrange("p n j -> p (n j)"))

        def quantize_h(b):
            quantize("h", b, work, live["hg", b][:].rearrange("p j r t -> p (j r t)"))

        def cols(i):
            return slice(i * P, (i + 1) * P)

        def stage1(b, j):
            a_codes, a_scales = live["a", b]
            v_codes, v_scales = live["v", b]
            hp = ring.tile([P, PACK, P], H_BANK_DTYPE, tag="ring", name="hp%d_%d" % (b, j))
            for t in range(PACK):
                nc.tensor.matmul_mx(
                    out=hp[:, t, :],
                    lhsT=v_codes[:, cols(t)].bitcast(FP8X4),
                    lhsT_scale=v_scales[:, cols(t)],
                    rhs=a_codes[:, cols(j)].bitcast(FP8X4),
                    rhs_scale=a_scales[:, cols(j)],
                    start=True,
                    stop=True,
                )
            if j == 0:
                live["hg", b] = work.tile([P, NT, P, PACK], BF16, tag="hg", name="hg%d" % b, align_bytes=64)
            nc.scalar.activation(out=live["hg", b][:, j, :, :], in_=hp[:].rearrange("p t r -> p r t"), func=RELU)

        def width(b, o):
            return L - P * TURNED[b] if o == 2 else L

        def project(b, o, j):
            h_codes, h_scales = live["h", b]
            w_codes, w_scales = live["w", o]
            n = width(b, o)
            acc = psum_o.tile([P, L], F32, tag="acc", name="acc%d_%d_%d" % (b, o, j))
            live["acc", b, o, j] = acc
            nc.tensor.matmul_mx(
                out=acc[:, 0:n],
                lhsT=h_codes[:, cols(j)].bitcast(FP8X4),
                lhsT_scale=h_scales[:, cols(j)],
                rhs=w_codes[:, 0:n].bitcast(FP8X4),
                rhs_scale=w_scales[:, 0:n],
                start=True,
                stop=True,
            )

        def staging(b, o):
            if ("st", b, o) not in live:
                live["st", b, o] = stage.tile([P, NT, L], F32, tag="st", name="st%d_%d" % (b, o))
            return live["st", b, o]

        def add_bias_and_store(b, o, j):
            st = staging(b, o)
            n = width(b, o)
            rows = None
            nc.vector.tensor_tensor(out=st[:, j, 0:n], in0=live["acc", b, o, j][:, 0:n], in1=bias_all[:, o, 0:n], op=ADD)
            first = 0
            for count in STORES[b][o]:
                if first + count == j + 1:
                    rows = slice(first, j + 1)
                first += count
            if rows is not None:
                nc.sync.dma_start(out=outs[o][b].rearrange("(p j) n -> p j n", j=NT)[:, rows, :], in_=st[:, rows, :])

        def turned_tiles(b):
            return range(NT - TURNED[b], NT)

        def project_turned(b, c):
            h_codes, h_scales = live["h", b]
            w_codes, w_scales = live["w", 2]
            bank = ring.tile([P, S], F32, tag="ring", name="tp%d_%d" % (b, c))
            nc.tensor.matmul_mx(
                out=bank[:],
                lhsT=w_codes[:, cols(c)].bitcast(FP8X4),
                lhsT_scale=w_scales[:, cols(c)],
                rhs=h_codes[:].bitcast(FP8X4),
                rhs_scale=h_scales[:],
                start=True,
                stop=True,
            )
            ot = work.tile([P, S], F32, tag="ot", name="ot%d_%d" % (b, c), bufs=4)
            live["ot", b, c] = ot
            nc.scalar.activation(out=ot[:], in_=bank[:], func=IDENTITY, bias=bias_col[:, c : c + 1])

        def turn_back(b, c):
            back = ring.tile([P, NT, P], F32, tag="ring", name="tb%d_%d" % (b, c))
            for j in range(NT):
                nc.tensor.transpose(back[:, j, :], live["ot", b, c][:, cols(j)], ident[:])
            nc.scalar.copy(out=staging(b, 2)[:, :, cols(c)], in_=back[:])

        fence = keep.tile([P, 1], U32, name="fence")

        def gpsimd_waits_for(kind, idx):
            nc.gpsimd.tensor_copy(out=fence[:], in_=live[kind, idx][0][:, 0:1])

        def spread_bias(first, count):
            bias_bank = ring.tile([P, count, L], BF16, tag="ring", name="bias_bank%d" % first)
            for i in range(count):
                nc.tensor.matmul(out=bias_bank[:, i, :], lhsT=ones[:], rhs=bias_rows[:, first + i, :], start=True, stop=True)
            nc.scalar.copy(
                out=bias_all[:, first : first + count, :].rearrange("p o n -> p (o n)").bitcast(F32),
                in_=bias_bank[:].rearrange("p o n -> p (o n)").bitcast(F32),
            )

        def keep_warm(name):
            dummy = psum_o.tile([P, L], F32, tag="acc", name="dummy" + name)
            nc.tensor.matmul(out=dummy[:], lhsT=ones[:], rhs=zeros[:], start=True, stop=True)

        for i in range(WARM):
            keep_warm("%d" % i)
        interleave_v_columns(0, nc.vector.tensor_copy, 0, V0_SPLIT)
        interleave_v_columns(0, nc.scalar.copy, V0_SPLIT, P)
        quantize_v(0)
        turn_attn(0, 0)
        turn_attn(0, 1)
        quantize_attn(0, 0, 2)
        stage1(0, 0)
        stage1(0, 1)
        quantize_attn(0, 1, 2)
        interleave_w(0, nc.vector.tensor_copy)
        stage1(0, 2)
        stage1(0, 3)
        spread_bias(0, 2)
        interleave_w(1, nc.vector.tensor_copy)
        quantize_w(0)
        for i in range(WARM):
            keep_warm("h%d" % i)
        quantize_w(1)
        quantize_h(0)
        for k in range(4):
            project(0, k // NT, k % NT)
        interleave_v(1, nc.vector.tensor_copy, 0, 2)
        gpsimd_waits_for("h", 0)
        interleave_v(1, gpsimd_copy, 2, 4)
        interleave_w(2, nc.scalar.copy)
        transpose_attn(1)
        copy_attn(1)
        spread_bias(2, 1)
        bias_col_bank = ring.tile([P, NT], F32, tag="ring", name="bias_col_bank")
        for c in range(NT):
            nc.tensor.matmul(out=bias_col_bank[:, c : c + 1], lhsT=bias_rows[:, 2, cols(c)], rhs=ones[:, 0:1], start=True, stop=True)
        bias_col = keep.tile([P, NT], F32, name="bias_col")
        nc.scalar.copy(out=bias_col[:], in_=bias_col_bank[:])

        per_set = 3 * NT
        for b in range(B):
            if 0 < b < B - 1:
                stage1(b + 1, 0)
                stage1(b + 1, 1)
            last = b + 2 >= B
            k2, k3 = (4, 5) if b == 0 else (1, 2)
            for k in range(per_set):
                add_bias_and_store(b, k // NT, k % NT)
                if k + 4 < per_set:
                    project(b, (k + 4) // NT, (k + 4) % NT)
                elif 0 < b and not last and b not in LATE:
                    keep_warm("%d_%d" % (b, k))
                if k == (BACK_AT if b > 0 and b not in LATE else 7):
                    for c in turned_tiles(b):
                        turn_back(b, c)
                if b == 0 and k == 3:
                    quantize_w(2)
                    quantize_v(1)
                    quantize_attn(1)
                    interleave_v(2, nc.scalar.copy, 0, 1)
                    gpsimd_waits_for("a", 1)
                    interleave_v(2, gpsimd_copy, 1, 4)
                    for c in turned_tiles(0):
                        project_turned(0, c)
                    stage1(1, 0)
                    stage1(1, 1)
                if b == 0 and k == 6:
                    transpose_attn(2)
                    copy_attn(2)
                if b + 1 < B and k == k2:
                    stage1(b + 1, 2)
                if b + 1 < B and k == k3:
                    stage1(b + 1, 3)
                    if b in LATE:
                        for c in turned_tiles(b):
                            project_turned(b, c)
                if b + 3 < B and k == (7 if b > 0 else 9):
                    transpose_attn(b + 3)
                    copy_attn(b + 3)
                if last and b + 1 < B:
                    if k == 9:
                        quantize_h(b + 1)
                        project(b + 1, 0, 0)
                        project(b + 1, 0, 1)
                    if k == 10:
                        project(b + 1, 0, 2)
                    if k == 11:
                        project(b + 1, 0, 3)
                        for c in turned_tiles(b + 1):
                            project_turned(b + 1, c)
            if not last:
                quantize_h(b + 1)
                for j in range(NT):
                    project(b + 1, 0, j)
                if b + 1 not in LATE:
                    for c in turned_tiles(b + 1):
                        project_turned(b + 1, c)
                quantize_v(b + 2)
                quantize_attn(b + 2)
                if b + 3 < B:
                    gpsimd_waits_for("a", b + 2)
                    interleave_v(b + 3, gpsimd_copy)
